import numpy as np
import ml_dtypes


def mxq(x, axis, fmt="e4m3"):
    dtype, down = {"e4m3": (ml_dtypes.float8_e4m3fn, 7), "e5m2": (ml_dtypes.float8_e5m2, 14)}[fmt]
    v = np.moveaxis(np.asarray(x, np.float32).astype(ml_dtypes.bfloat16).astype(np.float64), axis, -1)
    blocks = v.reshape(v.shape[:-1] + (-1, 32))
    amax = np.abs(blocks).max(-1, keepdims=True)
    byte = np.maximum(np.where(amax > 0, np.frexp(amax)[1] - 1 + 127, 0) - down, 1)
    scale = np.exp2(byte - 127.0)
    codes = (blocks / scale).astype(np.float32).astype(dtype).astype(np.float64)
    return np.moveaxis((codes * scale).reshape(v.shape), -1, axis)


WIDE = False


def mx_kscale(k):
    if not WIDE:
        return np.ones(k)
    levels = np.array([10, -10, 5, -5, 0])
    if k % 512:
        return np.exp2(np.random.permutation(np.resize(levels, k // 32))).repeat(32)
    a = np.empty((k // 512, 16))
    for p in range(k // 512):
        a[p, :8] = np.random.permutation(np.resize(levels, 8))
        for g in range(8):
            far = levels[np.abs(levels - a[p, g]) >= 10]
            a[p, g + 8] = far[np.random.randint(len(far))]
    return np.exp2(a.ravel()).repeat(32)


BF16 = ml_dtypes.bfloat16


def bf(x):
    return np.asarray(x, np.float32).astype(BF16)


def f64(x):
    return np.asarray(x).astype(np.float64)


B, IN, H, Z, G = 8192, 512, 128, 128, 4


def setup_inputs():
    s = mx_kscale(IN)
    return {"src_x": bf(np.random.standard_normal((B, IN)) * s),
            "zx": bf(np.random.standard_normal((B, G, Z))),
            "dx_w": bf(np.random.standard_normal((G, H, Z)) / np.sqrt(Z)),
            "w_x": bf(np.random.standard_normal((G, H, IN)) / np.sqrt(IN) / s)}


def reference(src_x, zx, dx_w, w_x):
    d_x = (f64(zx).transpose(1, 0, 2) @ f64(dx_w).transpose(0, 2, 1)).transpose(1, 0, 2)
    wx = (mxq(f64(src_x), 1, "e4m3") @ mxq(f64(w_x).reshape(G * H, IN), 1, "e4m3").T).reshape(B, G, H)
    return d_x * wx

@@ -1,0 +1,221 @@
+from contextlib import ExitStack
+
+import concourse.mybir as mybir
+from concourse.masks import make_identity
+
+BF16 = mybir.dt.bfloat16
+F32 = mybir.dt.float32
+U32 = mybir.dt.uint32
+U8 = mybir.dt.uint8
+FP8X4 = mybir.dt.float8_e4m3fn_x4
+
+P = 128
+B, IN, H, Z, G = 8192, 512, 128, 128, 4
+FLOPS = 2 * B * IN * G * H + 2 * B * G * H * Z
+ROW = 512
+WORDS = ROW // 2
+NT = B // P
+GT = 2
+NG = NT // GT
+
+LOAD_PIECES = (2, 2, 2, 2, 4, 4, 8, 8, 16, 16)
+FIRST_STORES = 2
+STORE_PIECES = (8, 8, 8, 8, 8, 4, 4, 4, 4, 2, 2, 2, 1, 1)
+OUT_TILES = 8
+X_COPY_ON_SCALAR_EVERY = 4
+
+
+def tile_metalstmcell_pa_t_kernel(tc, src_x, zx, dx_w, w_x, out):
+    nc = tc.nc
+    x_rows = src_x.rearrange("(p t) k -> p (t k)", t=NT)
+    z_rows = zx.rearrange("(p t) g z -> p (t g z)", t=NT)
+    out_rows = out.rearrange("(p t) g h -> p (t g h)", t=NT)
+
+    with ExitStack() as ctx:
+        const = ctx.enter_context(tc.tile_pool(name="const", bufs=1))
+        inputs = ctx.enter_context(tc.tile_pool(name="inputs", bufs=1))
+        work = ctx.enter_context(tc.tile_pool(name="work", bufs=3))
+        results = ctx.enter_context(tc.tile_pool(name="results", bufs=4))
+        psum = ctx.enter_context(tc.psum_pool(name="psum", bufs=2))
+        ctx.enter_context(tc.manual_schedule())
+
+        ident_b = const.tile([P, P], BF16, name="ident_b")
+        make_identity(nc, ident_b[:])
+        ident_f = const.tile([P, P], F32, name="ident_f")
+        make_identity(nc, ident_f[:])
+
+        x_sb = []
+        z_sb = []
+        place = {}
+        for i, n in enumerate(LOAD_PIECES):
+            x_sb.append(inputs.tile([P, n * ROW], BF16, name="x%d" % i))
+            z_sb.append(inputs.tile([P, n * ROW], BF16, name="z%d" % i))
+            for t in range(n):
+                place[len(place)] = (i, t)
+
+        def load(i):
+            lo = sum(LOAD_PIECES[:i]) * ROW
+            hi = lo + LOAD_PIECES[i] * ROW
+            nc.sync.dma_start(out=x_sb[i][:], in_=x_rows[:, lo:hi])
+            nc.sync.dma_start(out=z_sb[i][:], in_=z_rows[:, lo:hi])
+
+        dw_sb = const.tile([P, G * Z], BF16, name="dw_sb")
+        w_sb = const.tile([P, G * IN], BF16, name="w_sb")
+        nc.sync.dma_start(out=dw_sb[:].rearrange("h (g z) -> h g z", g=G), in_=dx_w.rearrange("g h z -> h g z"))
+        load(0)
+        nc.sync.dma_start(out=w_sb[:].rearrange("h (g k) -> h g k", g=G), in_=w_x.rearrange("g h k -> h g k"))
+        for i in range(1, len(LOAD_PIECES) - 1):
+            load(i)
+
+        x_bank = {}
+        z_bank = {}
+        x_pairs = {}
+        z_t = {}
+        x_mx = {}
+        d_bank = {}
+        d_sb = {}
+
+        def word_transposes(bank, words, first_word):
+            for a in range(GT):
+                for u in range(2):
+                    lo = first_word + a * WORDS
+                    nc.tensor.transpose(bank[:, a, u, :], words[:, lo + u:lo + WORDS:2], ident_f[:])
+
+        def pair_words(copy, dst, bank):
+            copy(out=dst.bitcast(F32).rearrange("p (a r u) -> p a r u", a=GT, u=2),
+                 in_=bank[:].rearrange("p a u r -> p a r u"))
+
+        def transpose_x(j):
+            i, t = place[j * GT]
+            x_bank[j] = psum.tile([P, GT, 2, P], F32, name="xp", tag="xp")
+            word_transposes(x_bank[j], x_sb[i][:].bitcast(F32), t * WORDS)
+
+        def open_z(j):
+            z_bank[j] = psum.tile([P, GT * ROW], BF16, name="zp", tag="zp")
+
+        def transpose_z(j, a, g):
+            i, t = place[j * GT + a]
+            lo = a * ROW + g * P
+            nc.tensor.transpose(z_bank[j][:, lo:lo + P], z_sb[i][:, t * ROW + g * Z:t * ROW + (g + 1) * Z],
+                                ident_b[:])
+
+        def copy_x(j):
+            x_pairs[j] = work.tile([P, GT * P * 4], BF16, name="xg", tag="xg", align_bytes=64)
+            on_scalar = j % X_COPY_ON_SCALAR_EVERY == 2
+            pair_words(nc.scalar.copy if on_scalar else nc.vector.tensor_copy, x_pairs[j][:], x_bank[j])
+
+        def copy_z(j):
+            z_t[j] = work.tile([P, GT * ROW], BF16, name="zt", tag="zt")
+            nc.scalar.copy(out=z_t[j][:].bitcast(F32), in_=z_bank[j][:].bitcast(F32))
+
+        def quantise(j):
+            codes = work.tile([P, GT * P], U32, name="xc", tag="xc", align_bytes=64)
+            scales = work.tile([P, GT * P], U8, name="xs", tag="xs", align_bytes=64)
+            nc.vector.quantize_mx(out=codes[:].bitcast(FP8X4), scales=scales[:], in_=x_pairs[j][:])
+            x_mx[j] = (codes, scales)
+
+        def open_d(j, a):
+            d_bank[(j, a)] = psum.tile([P, ROW], F32, name="dp", tag="dp")
+
+        def scaling_matmul(j, a, g):
+            lo = a * ROW + g * P
+            nc.tensor.matmul(d_bank[(j, a)][:, g * H:(g + 1) * H], lhsT=z_t[j][:, lo:lo + P],
+                             rhs=dw_t[:, g * H:(g + 1) * H], start=True, stop=True)
+
+        def copy_scalings(j):
+            for a in range(GT):
+                d_sb[(j, a)] = work.tile([P, ROW], F32, name="ds", tag="ds", bufs=4)
+                nc.scalar.copy(out=d_sb[(j, a)][:], in_=d_bank[(j, a)][:])
+
+        def projections(j):
+            codes, scales = x_mx[j]
+            banks = []
+            for a in range(GT):
+                bank = psum.tile([P, ROW], F32, name="wp", tag="wp")
+                nc.tensor.matmul_mx(out=bank[:], lhsT=codes[:, a * P:(a + 1) * P].bitcast(FP8X4),
+                                    lhsT_scale=scales[:, a * P:(a + 1) * P],
+                                    rhs=w_codes[:].bitcast(FP8X4), rhs_scale=w_scales[:], start=True, stop=True)
+                banks.append(bank)
+            return banks
+
+        dw_bank = psum.tile([P, GT * ROW], BF16, name="zp", tag="zp")
+        for g in range(G):
+            nc.tensor.transpose(dw_bank[:, g * H:(g + 1) * H], dw_sb[:, g * Z:(g + 1) * Z], ident_b[:])
+        dw_t = const.tile([P, G * H], BF16, name="dw_t")
+        nc.scalar.copy(out=dw_t[:].bitcast(F32), in_=dw_bank[:, 0:G * H].bitcast(F32))
+
+        def transpose_group(j):
+            transpose_x(j)
+            open_z(j)
+            for a in range(GT):
+                for g in range(G):
+                    transpose_z(j, a, g)
+            copy_x(j)
+            copy_z(j)
+
+        transpose_group(0)
+        w_pairs = const.tile([P, G * H * 4], BF16, name="w_pairs", align_bytes=64)
+        for q in range(2):
+            w_bank = psum.tile([P, GT, 2, P], F32, name="xp", tag="xp")
+            word_transposes(w_bank, w_sb[:].bitcast(F32), q * GT * WORDS)
+            pair_words(nc.vector.tensor_copy if q else nc.scalar.copy,
+                       w_pairs[:, q * GT * P * 4:(q + 1) * GT * P * 4], w_bank)
+        quantise(0)
+        transpose_group(1)
+        w_codes = const.tile([P, G * H], U32, name="w_codes", align_bytes=64)
+        w_scales = const.tile([P, G * H], U8, name="w_scales", align_bytes=64)
+        nc.vector.quantize_mx(out=w_codes[:].bitcast(FP8X4), scales=w_scales[:], in_=w_pairs[:])
+        open_z(2)
+        for a in range(GT):
+            for g in range(G):
+                transpose_z(2, a, g)
+        for a in range(GT):
+            open_d(0, a)
+            for g in range(G):
+                scaling_matmul(0, a, g)
+        copy_scalings(0)
+
+        store_ends = [sum(STORE_PIECES[:i + 1]) for i in range(len(STORE_PIECES))]
+        stored = 0
+        for j in range(NG):
+            ahead = j + 2 < NG
+            following = j + 1 < NG
+            further = j + 3 < NG
+            if ahead:
+                transpose_x(j + 2)
+                copy_z(j + 2)
+                copy_x(j + 2)
+            if following:
+                quantise(j + 1)
+                open_d(j + 1, 0)
+            if further:
+                open_z(j + 3)
+            for g in range(G):
+                if further:
+                    transpose_z(j + 3, 0, g)
+                if following:
+                    scaling_matmul(j + 1, 0, g)
+            w_banks = projections(j)
+            if following:
+                open_d(j + 1, 1)
+            for g in range(G):
+                if following:
+                    scaling_matmul(j + 1, 1, g)
+                if further:
+                    transpose_z(j + 3, 1, g)
+            if following:
+                copy_scalings(j + 1)
+            for a in range(GT):
+                t = j * GT + a
+                at = t % OUT_TILES
+                if at == 0:
+                    res = results.tile([P, OUT_TILES * ROW], F32, name="res", tag="res")
+                nc.vector.tensor_tensor(out=res[:, at * ROW:(at + 1) * ROW], in0=w_banks[a][:],
+                                        in1=d_sb[(j, a)][:], op=mybir.AluOpType.mult)
+                if t + 1 == store_ends[stored]:
+                    n = STORE_PIECES[stored]
+                    nc.sync.dma_start(out=out_rows[:, (t + 1 - n) * ROW:(t + 1) * ROW],
+                                      in_=res[:, (at + 1 - n) * ROW:(at + 1) * ROW])
+                    stored += 1
+                    if stored == FIRST_STORES:
+                        load(len(LOAD_PIECES) - 1)

@@ -56,14 +56,18 @@ def tile_metalstmcell_pa_t_kernel(tc, src_x, zx, dx_w, w_x, out):
         def load(i):
             lo = sum(LOAD_PIECES[:i]) * ROW
             hi = lo + LOAD_PIECES[i] * ROW
-            nc.sync.dma_start(out=x_sb[i][:], in_=x_rows[:, lo:hi])
             nc.sync.dma_start(out=z_sb[i][:], in_=z_rows[:, lo:hi])
+            nc.sync.dma_start(out=x_sb[i][:], in_=x_rows[:, lo:hi])
 
         dw_sb = const.tile([P, G * Z], BF16, name="dw_sb")
-        w_sb = const.tile([P, G * IN], BF16, name="w_sb")
+        w_sb = []
+        for q in range(2):
+            w_sb.append(const.tile([P, GT * IN], BF16, name="w_sb%d" % q))
         nc.sync.dma_start(out=dw_sb[:].rearrange("h (g z) -> h g z", g=G), in_=dx_w.rearrange("g h z -> h g z"))
         load(0)
-        nc.sync.dma_start(out=w_sb[:].rearrange("h (g k) -> h g k", g=G), in_=w_x.rearrange("g h k -> h g k"))
+        for q in range(2):
+            nc.sync.dma_start(out=w_sb[q][:].rearrange("h (g k) -> h g k", g=GT),
+                              in_=w_x[q * GT:(q + 1) * GT].rearrange("g h k -> h g k"))
         for i in range(1, len(LOAD_PIECES) - 1):
             load(i)
 
@@ -138,45 +142,71 @@ def tile_metalstmcell_pa_t_kernel(tc, src_x, zx, dx_w, w_x, out):
                 banks.append(bank)
             return banks
 
+        def transpose_whole_z(j):
+            open_z(j)
+            for a in range(GT):
+                for g in range(G):
+                    transpose_z(j, a, g)
+
+        def scalings(j):
+            for a in range(GT):
+                open_d(j, a)
+                for g in range(G):
+                    scaling_matmul(j, a, g)
+
+        store_ends = [sum(STORE_PIECES[:i + 1]) for i in range(len(STORE_PIECES))]
+        stores = []
+        res = {}
+
+        def product(j, a, bank):
+            t = j * GT + a
+            at = t % OUT_TILES
+            if at == 0:
+                res[t // OUT_TILES] = results.tile([P, OUT_TILES * ROW], F32, name="res", tag="res")
+            buf = res[t // OUT_TILES]
+            nc.vector.tensor_tensor(out=buf[:, at * ROW:(at + 1) * ROW], in0=bank[:],
+                                    in1=d_sb[(j, a)][:], op=mybir.AluOpType.mult)
+            if t + 1 == store_ends[len(stores)]:
+                n = STORE_PIECES[len(stores)]
+                nc.sync.dma_start(out=out_rows[:, (t + 1 - n) * ROW:(t + 1) * ROW],
+                                  in_=buf[:, (at + 1 - n) * ROW:(at + 1) * ROW])
+                stores.append(t)
+                if len(stores) == FIRST_STORES:
+                    load(len(LOAD_PIECES) - 1)
+
         dw_bank = psum.tile([P, GT * ROW], BF16, name="zp", tag="zp")
         for g in range(G):
             nc.tensor.transpose(dw_bank[:, g * H:(g + 1) * H], dw_sb[:, g * Z:(g + 1) * Z], ident_b[:])
         dw_t = const.tile([P, G * H], BF16, name="dw_t")
         nc.scalar.copy(out=dw_t[:].bitcast(F32), in_=dw_bank[:, 0:G * H].bitcast(F32))
 
-        def transpose_group(j):
-            transpose_x(j)
-            open_z(j)
-            for a in range(GT):
-                for g in range(G):
-                    transpose_z(j, a, g)
-            copy_x(j)
-            copy_z(j)
-
-        transpose_group(0)
-        w_pairs = const.tile([P, G * H * 4], BF16, name="w_pairs", align_bytes=64)
-        for q in range(2):
-            w_bank = psum.tile([P, GT, 2, P], F32, name="xp", tag="xp")
-            word_transposes(w_bank, w_sb[:].bitcast(F32), q * GT * WORDS)
-            pair_words(nc.vector.tensor_copy if q else nc.scalar.copy,
-                       w_pairs[:, q * GT * P * 4:(q + 1) * GT * P * 4], w_bank)
+        transpose_whole_z(0)
+        copy_z(0)
+        transpose_x(0)
+        copy_x(0)
         quantise(0)
-        transpose_group(1)
+        w_pairs = const.tile([P, G * H * 4], BF16, name="w_pairs", align_bytes=64)
         w_codes = const.tile([P, G * H], U32, name="w_codes", align_bytes=64)
         w_scales = const.tile([P, G * H], U8, name="w_scales", align_bytes=64)
-        nc.vector.quantize_mx(out=w_codes[:].bitcast(FP8X4), scales=w_scales[:], in_=w_pairs[:])
-        open_z(2)
-        for a in range(GT):
-            for g in range(G):
-                transpose_z(2, a, g)
-        for a in range(GT):
-            open_d(0, a)
-            for g in range(G):
-                scaling_matmul(0, a, g)
+        for q in range(2):
+            cols = slice(q * GT * P, (q + 1) * GT * P)
+            pairs = w_pairs[:, q * GT * P * 4:(q + 1) * GT * P * 4]
+            w_bank = psum.tile([P, GT, 2, P], F32, name="xp", tag="xp")
+            word_transposes(w_bank, w_sb[q][:].bitcast(F32), 0)
+            pair_words(nc.vector.tensor_copy if q else nc.scalar.copy, pairs, w_bank)
+            nc.vector.quantize_mx(out=w_codes[:, cols].bitcast(FP8X4), scales=w_scales[:, cols], in_=pairs)
+        scalings(0)
         copy_scalings(0)
+        transpose_whole_z(1)
+        copy_z(1)
+        transpose_x(1)
+        copy_x(1)
+        first_banks = projections(0)
+        product(0, 0, first_banks[0])
+        quantise(1)
+        product(0, 1, first_banks[1])
+        transpose_whole_z(2)
 
-        store_ends = [sum(STORE_PIECES[:i + 1]) for i in range(len(STORE_PIECES))]
-        stored = 0
         for j in range(NG):
             ahead = j + 2 < NG
             following = j + 1 < NG
@@ -186,7 +216,8 @@ def tile_metalstmcell_pa_t_kernel(tc, src_x, zx, dx_w, w_x, out):
                 copy_z(j + 2)
                 copy_x(j + 2)
             if following:
-                quantise(j + 1)
+                if j:
+                    quantise(j + 1)
                 open_d(j + 1, 0)
             if further:
                 open_z(j + 3)
@@ -195,7 +226,8 @@ def tile_metalstmcell_pa_t_kernel(tc, src_x, zx, dx_w, w_x, out):
                     transpose_z(j + 3, 0, g)
                 if following:
                     scaling_matmul(j + 1, 0, g)
-            w_banks = projections(j)
+            if j:
+                w_banks = projections(j)
             if following:
                 open_d(j + 1, 1)
             for g in range(G):
@@ -205,17 +237,6 @@ def tile_metalstmcell_pa_t_kernel(tc, src_x, zx, dx_w, w_x, out):
                     transpose_z(j + 3, 1, g)
             if following:
                 copy_scalings(j + 1)
-            for a in range(GT):
-                t = j * GT + a
-                at = t % OUT_TILES
-                if at == 0:
-                    res = results.tile([P, OUT_TILES * ROW], F32, name="res", tag="res")
-                nc.vector.tensor_tensor(out=res[:, at * ROW:(at + 1) * ROW], in0=w_banks[a][:],
-                                        in1=d_sb[(j, a)][:], op=mybir.AluOpType.mult)
-                if t + 1 == store_ends[stored]:
-                    n = STORE_PIECES[stored]
-                    nc.sync.dma_start(out=out_rows[:, (t + 1 - n) * ROW:(t + 1) * ROW],
-                                      in_=res[:, (at + 1 - n) * ROW:(at + 1) * ROW])
-                    stored += 1
-                    if stored == FIRST_STORES:
-                        load(len(LOAD_PIECES) - 1)
+            if j:
+                for a in range(GT):
+                    product(j, a, w_banks[a])

@@ -18,10 +18,9 @@ NT = B // P
 GT = 2
 NG = NT // GT
 
-LOAD_PIECES = (2, 2, 2, 2, 4, 4, 8, 8, 16, 16)
-FIRST_STORES = 2
-STORE_PIECES = (8, 8, 8, 8, 8, 4, 4, 4, 4, 2, 2, 2, 1, 1)
-OUT_TILES = 8
+LOAD_PIECES = (2, 2, 2, 4, 6, 10, 16, 22)
+STORE_PIECES = (16, 16, 8, 8, 4, 4, 4, 2, 1, 1)
+EARLY = NT // 2
 X_COPY_ON_SCALAR_EVERY = 4
 
 
@@ -35,7 +34,7 @@ def tile_metalstmcell_pa_t_kernel(tc, src_x, zx, dx_w, w_x, out):
         const = ctx.enter_context(tc.tile_pool(name="const", bufs=1))
         inputs = ctx.enter_context(tc.tile_pool(name="inputs", bufs=1))
         work = ctx.enter_context(tc.tile_pool(name="work", bufs=3))
-        results = ctx.enter_context(tc.tile_pool(name="results", bufs=4))
+        splits = ctx.enter_context(tc.tile_pool(name="splits", bufs=3))
         psum = ctx.enter_context(tc.psum_pool(name="psum", bufs=2))
         ctx.enter_context(tc.manual_schedule())
 
@@ -45,32 +44,28 @@ def tile_metalstmcell_pa_t_kernel(tc, src_x, zx, dx_w, w_x, out):
         make_identity(nc, ident_f[:])
 
         x_sb = []
-        z_sb = []
+        z_sb = inputs.tile([P, NT * ROW], BF16, name="z_sb")
         place = {}
         for i, n in enumerate(LOAD_PIECES):
             x_sb.append(inputs.tile([P, n * ROW], BF16, name="x%d" % i))
-            z_sb.append(inputs.tile([P, n * ROW], BF16, name="z%d" % i))
             for t in range(n):
                 place[len(place)] = (i, t)
 
         def load(i):
             lo = sum(LOAD_PIECES[:i]) * ROW
             hi = lo + LOAD_PIECES[i] * ROW
-            nc.sync.dma_start(out=z_sb[i][:], in_=z_rows[:, lo:hi])
+            nc.sync.dma_start(out=z_sb[:, lo:hi], in_=z_rows[:, lo:hi])
             nc.sync.dma_start(out=x_sb[i][:], in_=x_rows[:, lo:hi])
 
         dw_sb = const.tile([P, G * Z], BF16, name="dw_sb")
-        w_sb = []
-        for q in range(2):
-            w_sb.append(const.tile([P, GT * IN], BF16, name="w_sb%d" % q))
-        nc.sync.dma_start(out=dw_sb[:].rearrange("h (g z) -> h g z", g=G), in_=dx_w.rearrange("g h z -> h g z"))
+        w_sb = const.tile([P, G * IN], BF16, name="w_sb")
+        nc.sync.dma_start(out=dw_sb[:], in_=dx_w.rearrange("g (q r) z -> (g q) (r z)", r=G))
         load(0)
-        for q in range(2):
-            nc.sync.dma_start(out=w_sb[q][:].rearrange("h (g k) -> h g k", g=GT),
-                              in_=w_x[q * GT:(q + 1) * GT].rearrange("g h k -> h g k"))
-        for i in range(1, len(LOAD_PIECES) - 1):
+        nc.sync.dma_start(out=w_sb[:], in_=w_x.rearrange("g (q r) k -> (g q) (r k)", r=G))
+        for i in range(1, len(LOAD_PIECES)):
             load(i)
 
+        x_split = {}
         x_bank = {}
         z_bank = {}
         x_pairs = {}
@@ -89,19 +84,32 @@ def tile_metalstmcell_pa_t_kernel(tc, src_x, zx, dx_w, w_x, out):
             copy(out=dst.bitcast(F32).rearrange("p (a r u) -> p a r u", a=GT, u=2),
                  in_=bank[:].rearrange("p a u r -> p a r u"))
 
+        def split_words(j):
+            i, t = place[j * GT]
+            x_split[j] = splits.tile([P, GT * ROW], BF16, name="xw", tag="xw")
+            nc.gpsimd.tensor_copy(
+                out=x_split[j][:].bitcast(F32).rearrange("p (a u w) -> p a u w", a=GT, u=2),
+                in_=x_sb[i][:, t * ROW:(t + GT) * ROW].bitcast(F32).rearrange("p (a w u) -> p a u w", a=GT, u=2))
+
         def transpose_x(j):
             i, t = place[j * GT]
             x_bank[j] = psum.tile([P, GT, 2, P], F32, name="xp", tag="xp")
-            word_transposes(x_bank[j], x_sb[i][:].bitcast(F32), t * WORDS)
+            if j in x_split:
+                words = x_split[j][:].bitcast(F32)
+                for a in range(GT):
+                    for u in range(2):
+                        lo = (a * 2 + u) * P
+                        nc.tensor.transpose(x_bank[j][:, a, u, :], words[:, lo:lo + P], ident_f[:])
+            else:
+                word_transposes(x_bank[j], x_sb[i][:].bitcast(F32), t * WORDS)
 
         def open_z(j):
             z_bank[j] = psum.tile([P, GT * ROW], BF16, name="zp", tag="zp")
 
         def transpose_z(j, a, g):
-            i, t = place[j * GT + a]
+            at = (j * GT + a) * ROW + g * Z
             lo = a * ROW + g * P
-            nc.tensor.transpose(z_bank[j][:, lo:lo + P], z_sb[i][:, t * ROW + g * Z:t * ROW + (g + 1) * Z],
-                                ident_b[:])
+            nc.tensor.transpose(z_bank[j][:, lo:lo + P], z_sb[:, at:at + Z], ident_b[:])
 
         def copy_x(j):
             x_pairs[j] = work.tile([P, GT * P * 4], BF16, name="xg", tag="xg", align_bytes=64)
@@ -154,31 +162,29 @@ def tile_metalstmcell_pa_t_kernel(tc, src_x, zx, dx_w, w_x, out):
                 for g in range(G):
                     scaling_matmul(j, a, g)
 
+        early = inputs.tile([P, EARLY * ROW], F32, name="early")
         store_ends = [sum(STORE_PIECES[:i + 1]) for i in range(len(STORE_PIECES))]
         stores = []
-        res = {}
+
+        def results(lo, hi):
+            if hi <= EARLY:
+                return early[:, lo * ROW:hi * ROW]
+            return z_sb[:].bitcast(F32)[:, (lo - EARLY) * ROW:(hi - EARLY) * ROW]
 
         def product(j, a, bank):
             t = j * GT + a
-            at = t % OUT_TILES
-            if at == 0:
-                res[t // OUT_TILES] = results.tile([P, OUT_TILES * ROW], F32, name="res", tag="res")
-            buf = res[t // OUT_TILES]
-            nc.vector.tensor_tensor(out=buf[:, at * ROW:(at + 1) * ROW], in0=bank[:],
-                                    in1=d_sb[(j, a)][:], op=mybir.AluOpType.mult)
+            nc.vector.tensor_tensor(out=results(t, t + 1), in0=bank[:], in1=d_sb[(j, a)][:], op=mybir.AluOpType.mult)
             if t + 1 == store_ends[len(stores)]:
                 n = STORE_PIECES[len(stores)]
-                nc.sync.dma_start(out=out_rows[:, (t + 1 - n) * ROW:(t + 1) * ROW],
-                                  in_=buf[:, (at + 1 - n) * ROW:(at + 1) * ROW])
+                nc.sync.dma_start(out=out_rows[:, (t + 1 - n) * ROW:(t + 1) * ROW], in_=results(t + 1 - n, t + 1))
                 stores.append(t)
-                if len(stores) == FIRST_STORES:
-                    load(len(LOAD_PIECES) - 1)
 
         dw_bank = psum.tile([P, GT * ROW], BF16, name="zp", tag="zp")
-        for g in range(G):
-            nc.tensor.transpose(dw_bank[:, g * H:(g + 1) * H], dw_sb[:, g * Z:(g + 1) * Z], ident_b[:])
+        for r in range(G):
+            nc.tensor.transpose(dw_bank[:, r * P:(r + 1) * P], dw_sb[:, r * Z:(r + 1) * Z], ident_b[:])
         dw_t = const.tile([P, G * H], BF16, name="dw_t")
-        nc.scalar.copy(out=dw_t[:].bitcast(F32), in_=dw_bank[:, 0:G * H].bitcast(F32))
+        nc.scalar.copy(out=dw_t[:].rearrange("z (p r) -> z p r", r=G),
+                       in_=dw_bank[:, 0:G * H].rearrange("z (r p) -> z p r", r=G))
 
         transpose_whole_z(0)
         copy_z(0)
@@ -189,12 +195,12 @@ def tile_metalstmcell_pa_t_kernel(tc, src_x, zx, dx_w, w_x, out):
         w_codes = const.tile([P, G * H], U32, name="w_codes", align_bytes=64)
         w_scales = const.tile([P, G * H], U8, name="w_scales", align_bytes=64)
         for q in range(2):
-            cols = slice(q * GT * P, (q + 1) * GT * P)
-            pairs = w_pairs[:, q * GT * P * 4:(q + 1) * GT * P * 4]
             w_bank = psum.tile([P, GT, 2, P], F32, name="xp", tag="xp")
-            word_transposes(w_bank, w_sb[q][:].bitcast(F32), 0)
-            pair_words(nc.vector.tensor_copy if q else nc.scalar.copy, pairs, w_bank)
-            nc.vector.quantize_mx(out=w_codes[:, cols].bitcast(FP8X4), scales=w_scales[:, cols], in_=pairs)
+            word_transposes(w_bank, w_sb[:].bitcast(F32), q * GT * WORDS)
+            copy = nc.vector.tensor_copy if q else nc.scalar.copy
+            copy(out=w_pairs[:].bitcast(F32).rearrange("k (p q a u) -> k q p a u", q=2, a=GT, u=2)[:, q],
+                 in_=w_bank[:].rearrange("k a u p -> k p a u"))
+        nc.vector.quantize_mx(out=w_codes[:].bitcast(FP8X4), scales=w_scales[:], in_=w_pairs[:])
         scalings(0)
         copy_scalings(0)
         transpose_whole_z(1)
@@ -211,6 +217,8 @@ def tile_metalstmcell_pa_t_kernel(tc, src_x, zx, dx_w, w_x, out):
             ahead = j + 2 < NG
             following = j + 1 < NG
             further = j + 3 < NG
+            if j + 4 < NG and j % 2 == 0:
+                split_words(j + 4)
             if ahead:
                 transpose_x(j + 2)
                 copy_z(j + 2)

from contextlib import ExitStack

import concourse.mybir as mybir
from concourse.masks import make_identity

BF16 = mybir.dt.bfloat16
F32 = mybir.dt.float32
U32 = mybir.dt.uint32
U8 = mybir.dt.uint8
FP8X4 = mybir.dt.float8_e4m3fn_x4

P = 128
B, IN, H, Z, G = 8192, 512, 128, 128, 4
FLOPS = 2 * B * IN * G * H + 2 * B * G * H * Z
ROW = 512
WORDS = ROW // 2
NT = B // P
GT = 2
NG = NT // GT

LOAD_PIECES = (2, 2, 2, 4, 6, 10, 16, 22)
STORE_PIECES = (16, 16, 8, 8, 4, 4, 4, 2, 1, 1)
EARLY = NT // 2
X_COPY_ON_SCALAR_EVERY = 4


def tile_metalstmcell_pa_t_kernel(tc, src_x, zx, dx_w, w_x, out):
    nc = tc.nc
    x_rows = src_x.rearrange("(p t) k -> p (t k)", t=NT)
    z_rows = zx.rearrange("(p t) g z -> p (t g z)", t=NT)
    out_rows = out.rearrange("(p t) g h -> p (t g h)", t=NT)

    with ExitStack() as ctx:
        const = ctx.enter_context(tc.tile_pool(name="const", bufs=1))
        inputs = ctx.enter_context(tc.tile_pool(name="inputs", bufs=1))
        work = ctx.enter_context(tc.tile_pool(name="work", bufs=3))
        splits = ctx.enter_context(tc.tile_pool(name="splits", bufs=3))
        psum = ctx.enter_context(tc.psum_pool(name="psum", bufs=2))
        ctx.enter_context(tc.manual_schedule())

        ident_b = const.tile([P, P], BF16, name="ident_b")
        make_identity(nc, ident_b[:])
        ident_f = const.tile([P, P], F32, name="ident_f")
        make_identity(nc, ident_f[:])

        x_sb = []
        z_sb = inputs.tile([P, NT * ROW], BF16, name="z_sb")
        place = {}
        for i, n in enumerate(LOAD_PIECES):
            x_sb.append(inputs.tile([P, n * ROW], BF16, name="x%d" % i))
            for t in range(n):
                place[len(place)] = (i, t)

        def load(i):
            lo = sum(LOAD_PIECES[:i]) * ROW
            hi = lo + LOAD_PIECES[i] * ROW
            nc.sync.dma_start(out=z_sb[:, lo:hi], in_=z_rows[:, lo:hi])
            nc.sync.dma_start(out=x_sb[i][:], in_=x_rows[:, lo:hi])

        dw_sb = const.tile([P, G * Z], BF16, name="dw_sb")
        w_sb = const.tile([P, G * IN], BF16, name="w_sb")
        nc.sync.dma_start(out=dw_sb[:], in_=dx_w.rearrange("g (q r) z -> (g q) (r z)", r=G))
        load(0)
        nc.sync.dma_start(out=w_sb[:], in_=w_x.rearrange("g (q r) k -> (g q) (r k)", r=G))
        for i in range(1, len(LOAD_PIECES)):
            load(i)

        x_split = {}
        x_bank = {}
        z_bank = {}
        x_pairs = {}
        z_t = {}
        x_mx = {}
        d_bank = {}
        d_sb = {}

        def word_transposes(bank, words, first_word):
            for a in range(GT):
                for u in range(2):
                    lo = first_word + a * WORDS
                    nc.tensor.transpose(bank[:, a, u, :], words[:, lo + u:lo + WORDS:2], ident_f[:])

        def pair_words(copy, dst, bank):
            copy(out=dst.bitcast(F32).rearrange("p (a r u) -> p a r u", a=GT, u=2),
                 in_=bank[:].rearrange("p a u r -> p a r u"))

        def split_words(j):
            i, t = place[j * GT]
            x_split[j] = splits.tile([P, GT * ROW], BF16, name="xw", tag="xw")
            nc.gpsimd.tensor_copy(
                out=x_split[j][:].bitcast(F32).rearrange("p (a u w) -> p a u w", a=GT, u=2),
                in_=x_sb[i][:, t * ROW:(t + GT) * ROW].bitcast(F32).rearrange("p (a w u) -> p a u w", a=GT, u=2))

        def transpose_x(j):
            i, t = place[j * GT]
            x_bank[j] = psum.tile([P, GT, 2, P], F32, name="xp", tag="xp")
            if j in x_split:
                words = x_split[j][:].bitcast(F32)
                for a in range(GT):
                    for u in range(2):
                        lo = (a * 2 + u) * P
                        nc.tensor.transpose(x_bank[j][:, a, u, :], words[:, lo:lo + P], ident_f[:])
            else:
                word_transposes(x_bank[j], x_sb[i][:].bitcast(F32), t * WORDS)

        def open_z(j):
            z_bank[j] = psum.tile([P, GT * ROW], BF16, name="zp", tag="zp")

        def transpose_z(j, a, g):
            at = (j * GT + a) * ROW + g * Z
            lo = a * ROW + g * P
            nc.tensor.transpose(z_bank[j][:, lo:lo + P], z_sb[:, at:at + Z], ident_b[:])

        def copy_x(j):
            x_pairs[j] = work.tile([P, GT * P * 4], BF16, name="xg", tag="xg", align_bytes=64)
            on_scalar = j % X_COPY_ON_SCALAR_EVERY == 2
            pair_words(nc.scalar.copy if on_scalar else nc.vector.tensor_copy, x_pairs[j][:], x_bank[j])

        def copy_z(j):
            z_t[j] = work.tile([P, GT * ROW], BF16, name="zt", tag="zt")
            nc.scalar.copy(out=z_t[j][:].bitcast(F32), in_=z_bank[j][:].bitcast(F32))

        def quantise(j):
            codes = work.tile([P, GT * P], U32, name="xc", tag="xc", align_bytes=64)
            scales = work.tile([P, GT * P], U8, name="xs", tag="xs", align_bytes=64)
            nc.vector.quantize_mx(out=codes[:].bitcast(FP8X4), scales=scales[:], in_=x_pairs[j][:])
            x_mx[j] = (codes, scales)

        def open_d(j, a):
            d_bank[(j, a)] = psum.tile([P, ROW], F32, name="dp", tag="dp")

        def scaling_matmul(j, a, g):
            lo = a * ROW + g * P
            nc.tensor.matmul(d_bank[(j, a)][:, g * H:(g + 1) * H], lhsT=z_t[j][:, lo:lo + P],
                             rhs=dw_t[:, g * H:(g + 1) * H], start=True, stop=True)

        def copy_scalings(j):
            for a in range(GT):
                d_sb[(j, a)] = work.tile([P, ROW], F32, name="ds", tag="ds", bufs=4)
                nc.scalar.copy(out=d_sb[(j, a)][:], in_=d_bank[(j, a)][:])

        def projections(j):
            codes, scales = x_mx[j]
            banks = []
            for a in range(GT):
                bank = psum.tile([P, ROW], F32, name="wp", tag="wp")
                nc.tensor.matmul_mx(out=bank[:], lhsT=codes[:, a * P:(a + 1) * P].bitcast(FP8X4),
                                    lhsT_scale=scales[:, a * P:(a + 1) * P],
                                    rhs=w_codes[:].bitcast(FP8X4), rhs_scale=w_scales[:], start=True, stop=True)
                banks.append(bank)
            return banks

        def transpose_whole_z(j):
            open_z(j)
            for a in range(GT):
                for g in range(G):
                    transpose_z(j, a, g)

        def scalings(j):
            for a in range(GT):
                open_d(j, a)
                for g in range(G):
                    scaling_matmul(j, a, g)

        early = inputs.tile([P, EARLY * ROW], F32, name="early")
        store_ends = [sum(STORE_PIECES[:i + 1]) for i in range(len(STORE_PIECES))]
        stores = []

        def results(lo, hi):
            if hi <= EARLY:
                return early[:, lo * ROW:hi * ROW]
            return z_sb[:].bitcast(F32)[:, (lo - EARLY) * ROW:(hi - EARLY) * ROW]

        def product(j, a, bank):
            t = j * GT + a
            nc.vector.tensor_tensor(out=results(t, t + 1), in0=bank[:], in1=d_sb[(j, a)][:], op=mybir.AluOpType.mult)
            if t + 1 == store_ends[len(stores)]:
                n = STORE_PIECES[len(stores)]
                nc.sync.dma_start(out=out_rows[:, (t + 1 - n) * ROW:(t + 1) * ROW], in_=results(t + 1 - n, t + 1))
                stores.append(t)

        dw_bank = psum.tile([P, GT * ROW], BF16, name="zp", tag="zp")
        for r in range(G):
            nc.tensor.transpose(dw_bank[:, r * P:(r + 1) * P], dw_sb[:, r * Z:(r + 1) * Z], ident_b[:])
        dw_t = const.tile([P, G * H], BF16, name="dw_t")
        nc.scalar.copy(out=dw_t[:].rearrange("z (p r) -> z p r", r=G),
                       in_=dw_bank[:, 0:G * H].rearrange("z (r p) -> z p r", r=G))

        transpose_whole_z(0)
        copy_z(0)
        transpose_x(0)
        copy_x(0)
        quantise(0)
        w_pairs = const.tile([P, G * H * 4], BF16, name="w_pairs", align_bytes=64)
        w_codes = const.tile([P, G * H], U32, name="w_codes", align_bytes=64)
        w_scales = const.tile([P, G * H], U8, name="w_scales", align_bytes=64)
        for q in range(2):
            w_bank = psum.tile([P, GT, 2, P], F32, name="xp", tag="xp")
            word_transposes(w_bank, w_sb[:].bitcast(F32), q * GT * WORDS)
            copy = nc.vector.tensor_copy if q else nc.scalar.copy
            copy(out=w_pairs[:].bitcast(F32).rearrange("k (p q a u) -> k q p a u", q=2, a=GT, u=2)[:, q],
                 in_=w_bank[:].rearrange("k a u p -> k p a u"))
        nc.vector.quantize_mx(out=w_codes[:].bitcast(FP8X4), scales=w_scales[:], in_=w_pairs[:])
        scalings(0)
        copy_scalings(0)
        transpose_whole_z(1)
        copy_z(1)
        transpose_x(1)
        copy_x(1)
        first_banks = projections(0)
        product(0, 0, first_banks[0])
        quantise(1)
        product(0, 1, first_banks[1])
        transpose_whole_z(2)

        for j in range(NG):
            ahead = j + 2 < NG
            following = j + 1 < NG
            further = j + 3 < NG
            if j + 4 < NG and j % 2 == 0:
                split_words(j + 4)
            if ahead:
                transpose_x(j + 2)
                copy_z(j + 2)
                copy_x(j + 2)
            if following:
                if j:
                    quantise(j + 1)
                open_d(j + 1, 0)
            if further:
                open_z(j + 3)
            for g in range(G):
                if further:
                    transpose_z(j + 3, 0, g)
                if following:
                    scaling_matmul(j + 1, 0, g)
            if j:
                w_banks = projections(j)
            if following:
                open_d(j + 1, 1)
            for g in range(G):
                if following:
                    scaling_matmul(j + 1, 1, g)
                if further:
                    transpose_z(j + 3, 1, g)
            if following:
                copy_scalings(j + 1)
            if j:
                for a in range(GT):
                    product(j, a, w_banks[a])
